import numpy as np
import ml_dtypes


def mxq(x, axis, fmt="e4m3"):
    dtype, down = {"e4m3": (ml_dtypes.float8_e4m3fn, 7), "e5m2": (ml_dtypes.float8_e5m2, 14)}[fmt]
    v = np.moveaxis(np.asarray(x, np.float32).astype(ml_dtypes.bfloat16).astype(np.float64), axis, -1)
    blocks = v.reshape(v.shape[:-1] + (-1, 32))
    amax = np.abs(blocks).max(-1, keepdims=True)
    byte = np.maximum(np.where(amax > 0, np.frexp(amax)[1] - 1 + 127, 0) - down, 1)
    scale = np.exp2(byte - 127.0)
    codes = (blocks / scale).astype(np.float32).astype(dtype).astype(np.float64)
    return np.moveaxis((codes * scale).reshape(v.shape), -1, axis)


WIDE = False


def mx_kscale(k):
    if not WIDE:
        return np.ones(k)
    levels = np.array([10, -10, 5, -5, 0])
    if k % 512:
        return np.exp2(np.random.permutation(np.resize(levels, k // 32))).repeat(32)
    a = np.empty((k // 512, 16))
    for p in range(k // 512):
        a[p, :8] = np.random.permutation(np.resize(levels, 8))
        for g in range(8):
            far = levels[np.abs(levels - a[p, g]) >= 10]
            a[p, g + 8] = far[np.random.randint(len(far))]
    return np.exp2(a.ravel()).repeat(32)


BF16 = ml_dtypes.bfloat16


def bf(x):
    return np.asarray(x, np.float32).astype(BF16)


def f64(x):
    return np.asarray(x).astype(np.float64)


B, D_IN, D_H = 512, 1024, 1024


def sigmoid(v):
    return 1.0 / (1.0 + np.exp(-v))


def draw0():
    s, t = mx_kscale(D_IN), mx_kscale(D_H)
    fg = np.exp(0.75 * np.random.standard_normal((B, D_H)))
    ig = np.exp(0.75 * np.random.standard_normal((B, D_H)))
    c = fg * np.random.standard_normal((B, D_H)) + ig * np.tanh(0.75 * np.random.standard_normal((B, D_H)))
    n = fg * np.random.uniform(size=(B, D_H)) + ig
    return {"x": bf(np.random.standard_normal((B, D_IN)) * s),
            "h_prev": bf(np.random.standard_normal((B, D_H)) * t),
            "c": bf(c),
            "n": bf(n),
            "W_o": bf(np.random.standard_normal((D_IN, D_H)) * 0.5 / np.sqrt(D_IN) / s[:, None]),
            "b_o": bf(np.random.standard_normal(D_H) * 0.3),
            "U_o": bf(np.random.standard_normal((D_H, D_H)) * 0.5 / np.sqrt(D_H) / t[:, None])}


def core(x, h_prev, c, n, W_o, b_o, U_o):
    o = sigmoid((mxq(f64(x), 1, "e4m3") @ mxq(f64(W_o), 0, "e4m3")) + f64(b_o) + (mxq(f64(h_prev), 1, "e4m3") @ mxq(f64(U_o), 0, "e4m3")))
    return o * (f64(c) / (f64(n) + 1e-6))


def e4m3fn_bytes(y):
    return np.clip(np.asarray(y, np.float64), -448.0, 448.0).astype(np.float32).astype(ml_dtypes.float8_e4m3fn).view(np.uint8)


def e4m3fn_values(b):
    return np.asarray(b, np.uint8).view(ml_dtypes.float8_e4m3fn).astype(np.float64)


def setup_inputs():
    d = draw0()
    x0 = np.asarray(d['W_o']).astype(np.float64)
    s = (np.max(np.abs(x0), axis=(1,), keepdims=True) / 448.0).astype(np.float32)
    out = {}
    for k, v in d.items():
        if k == 'W_o':
            out['W_o_bytes'] = e4m3fn_bytes(x0 / s.astype(np.float64))
            out['W_o_scale'] = s
        else:
            out[k] = v
    return out


def reference(x, h_prev, c, n, W_o_bytes, W_o_scale, b_o, U_o):
    return core(x, h_prev, c, n, e4m3fn_values(W_o_bytes) * W_o_scale.astype(np.float64), b_o, U_o)

@@ -1,0 +1,287 @@
+from contextlib import ExitStack
+
+import concourse.mybir as mybir
+from concourse.masks import make_identity
+
+B, D_IN, D_H = 512, 1024, 1024
+FLOPS = 2 * B * (D_IN + D_H) * D_H
+
+F32 = mybir.dt.float32
+BF16 = mybir.dt.bfloat16
+U32 = mybir.dt.uint32
+U8 = mybir.dt.uint8
+FP8 = mybir.dt.float8_e4m3fn
+FP8X4 = mybir.dt.float8_e4m3fn_x4
+ACT = mybir.ActivationFunctionType
+ALU = mybir.AluOpType
+
+P = 128
+PACK = 4
+K_PASS = P * PACK
+ROW_TILES = B // P
+CHUNK = 256
+N_CHUNKS = D_H // CHUNK
+HALF = 512
+EPS = 1e-6
+
+XCOPY = ("s", "s", "s", "s", "v", "v", "v", "v")
+
+
+def tile_slstmcell_pb_kernel(tc, x, h_prev, c, n, W_o_bytes, W_o_scale, b_o, U_o, out):
+    nc = tc.nc
+    with ExitStack() as ctx:
+        keep = ctx.enter_context(tc.tile_pool(name="keep", bufs=1))
+        rot = ctx.enter_context(tc.tile_pool(name="rot", bufs=3))
+        ps_acc = ctx.enter_context(tc.psum_pool(name="ps_acc", bufs=4))
+        ps_tp = ctx.enter_context(tc.psum_pool(name="ps_tp", bufs=4))
+        ctx.enter_context(tc.manual_schedule())
+
+        one = keep.tile([P, 1], F32, name="one")
+        nc.gpsimd.memset(one[:], 1.0)
+        scratch = keep.tile([P, 1], F32, name="scratch")
+        wsc = keep.tile([P, 2, PACK], F32, name="wsc")
+        nc.sync.dma_start(out=wsc[:], in_=W_o_scale.rearrange("(g p t) o -> p g (t o)", p=P, t=PACK))
+        b_sb = keep.tile([P, D_H // P], BF16, name="b_sb")
+        nc.scalar.activation(out=scratch[:], in_=one[:], func=ACT.Ln)
+        ident = keep.tile([P, P], F32, name="ident")
+        make_identity(nc, ident[:])
+        b_half = keep.tile([P, D_H // P], F32, name="b_half")
+
+        w_view = W_o_bytes.rearrange("(g p t) d -> g p t d", p=P, t=PACK)
+        u_view = U_o.rearrange("(g p t) d -> g p t d", p=P, t=PACK)
+        w8 = [keep.tile([P, 2, PACK, HALF], U8, name="w8_%d" % hf) for hf in range(2)]
+        u_raw = [keep.tile([P, 2, PACK, HALF], BF16, name="u_raw_%d" % hf) for hf in range(2)]
+        act_sb = {}
+        for name in ("x", "h", "n", "c"):
+            act_sb[name] = keep.tile([P, ROW_TILES, D_IN], BF16, name="%s_sb" % name)
+
+        def load_w(g, hf):
+            nc.sync.dma_start(out=w8[hf][:, g, :, :], in_=w_view[g][:, :, hf * HALF:(hf + 1) * HALF])
+
+        def load_u(g, hf):
+            nc.sync.dma_start(out=u_raw[hf][:, g, :, :], in_=u_view[g][:, :, hf * HALF:(hf + 1) * HALF])
+
+        def load_act(name, src, rp):
+            nc.sync.dma_start(
+                out=act_sb[name][:, 2 * rp:2 * rp + 2, :],
+                in_=src.rearrange("(i p) k -> p i k", p=P)[:, 2 * rp:2 * rp + 2, :],
+            )
+
+        load_w(0, 0)
+        load_u(0, 0)
+        load_w(1, 0)
+        load_u(1, 0)
+        load_act("x", x, 0)
+        load_act("x", x, 1)
+        load_act("h", h_prev, 0)
+        load_act("h", h_prev, 1)
+        load_w(0, 1)
+        load_w(1, 1)
+        load_u(0, 1)
+        load_u(1, 1)
+        with nc.allow_non_contiguous_dma(reason="bias: one element a partition, 1024 elements in all"):
+            nc.sync.dma_start(out=b_sb[:], in_=b_o.rearrange("(j p) -> p j", p=P))
+        nc.gpsimd.tensor_scalar(out=b_half[:], in0=b_sb[:], scalar1=0.5, scalar2=0.0, op0=ALU.mult, op1=ALU.add)
+        load_act("n", n, 0)
+        load_act("n", n, 1)
+        load_act("c", c, 0)
+        load_act("c", c, 1)
+
+        w_wide = [keep.tile([P, 2, PACK, HALF], BF16, name="w_wide_%d" % hf) for hf in range(2)]
+        wg = [keep.tile([P, 4, CHUNK, PACK], BF16, name="wg_%d" % k, align_bytes=64) for k in range(N_CHUNKS)]
+        wq = [keep.tile([P, 4 * CHUNK], U32, name="wq_%d" % k, align_bytes=64) for k in range(N_CHUNKS)]
+        ws = [keep.tile([P, 4 * CHUNK], U8, name="ws_%d" % k, align_bytes=64) for k in range(N_CHUNKS)]
+        xg = [keep.tile([P, 2 * B * PACK], BF16, name="xg_%d" % a, align_bytes=64) for a in range(2)]
+        xq = [keep.tile([P, 2 * B], U32, name="xq_%d" % a, align_bytes=64) for a in range(2)]
+        xs = [keep.tile([P, 2 * B], U8, name="xs_%d" % a, align_bytes=64) for a in range(2)]
+        log_n = keep.tile([P, ROW_TILES, D_H], F32, name="log_n")
+        ratio = [keep.tile([P, ROW_TILES, CHUNK], F32, name="ratio_%d" % k) for k in range(N_CHUNKS)]
+        o_sb = [keep.tile([P, ROW_TILES, CHUNK], F32, name="o_sb_%d" % k) for k in range(N_CHUNKS)]
+
+        def widen(hf, c0, width):
+            for g in range(2):
+                for t in range(PACK):
+                    nc.scalar.activation(
+                        out=w_wide[hf][:, g, t, c0:c0 + width],
+                        in_=w8[hf][:, g, t, c0:c0 + width].bitcast(FP8),
+                        func=ACT.Copy,
+                        scale=wsc[:, g, t:t + 1],
+                    )
+
+        def wint(k):
+            hf, c0 = divmod(k * CHUNK, HALF)
+            nc.vector.tensor_copy(
+                out=wg[k][:, 0:2, :, :],
+                in_=w_wide[hf][:, :, :, c0:c0 + CHUNK].rearrange("p g t d -> p g d t"),
+            )
+
+        def uint_g(k, g):
+            hf, c0 = divmod(k * CHUNK, HALF)
+            nc.vector.tensor_copy(
+                out=wg[k][:, 2 + g, :, :],
+                in_=u_raw[hf][:, g, :, c0:c0 + CHUNK].rearrange("p t d -> p d t"),
+            )
+
+        def uint(k):
+            hf, c0 = divmod(k * CHUNK, HALF)
+            nc.vector.tensor_copy(
+                out=wg[k][:, 2:4, :, :],
+                in_=u_raw[hf][:, :, :, c0:c0 + CHUNK].rearrange("p g t d -> p g d t"),
+            )
+
+        def quant_w(k):
+            nc.vector.quantize_mx(
+                out=wq[k][:].bitcast(FP8X4),
+                scales=ws[k][:],
+                in_=wg[k][:].rearrange("p q d t -> p (q d t)"),
+            )
+
+        banks = {}
+
+        def turn_act(name, g, rp):
+            bank = ps_tp.tile([P, 2, 2 * P], F32, name="bank", tag="tp")
+            banks[(name, g, rp)] = bank
+            for ii in range(2):
+                words = act_sb[name][:, 2 * rp + ii, :].bitcast(F32)
+                for u in range(2):
+                    nc.tensor.transpose(
+                        bank[:, u, ii * P:(ii + 1) * P],
+                        words[:, 256 * g + u:256 * (g + 1):2],
+                        ident[:],
+                    )
+
+        def copy_act(name, g, rp, engine):
+            a = 0 if name == "x" else 1
+            r0 = g * B + rp * 2 * P
+            dst = xg[a][:].bitcast(F32).rearrange("p (r u) -> p r u", u=2)[:, r0:r0 + 2 * P, :]
+            src = banks[(name, g, rp)][:].rearrange("p u r -> p r u")
+            if engine == "s":
+                nc.scalar.copy(out=dst, in_=src)
+            else:
+                nc.vector.tensor_copy(out=dst, in_=src)
+
+        def quant_x(a):
+            nc.vector.quantize_mx(out=xq[a][:].bitcast(FP8X4), scales=xs[a][:], in_=xg[a][:])
+
+        acc = {}
+        gate_t = {}
+        back = {}
+
+        def mx(j):
+            k, jj = divmod(j, 2)
+            acc[j] = ps_acc.tile([P, B], F32, name="acc", tag="acc")
+            for q in range(4):
+                cols = slice(q * CHUNK + jj * P, q * CHUNK + (jj + 1) * P)
+                nc.tensor.matmul_mx(
+                    out=acc[j][:],
+                    lhsT=wq[k][:, cols].bitcast(FP8X4),
+                    lhsT_scale=ws[k][:, cols],
+                    rhs=xq[q // 2][:, (q % 2) * B:(q % 2 + 1) * B].bitcast(FP8X4),
+                    rhs_scale=xs[q // 2][:, (q % 2) * B:(q % 2 + 1) * B],
+                    start=(q == 0),
+                    stop=(q == 3),
+                )
+
+        def tanh(j):
+            gate_t[j] = rot.tile([P, B], F32, name="gate_t", tag="gate_t")
+            nc.scalar.activation(out=gate_t[j][:], in_=acc[j][:], func=ACT.Tanh, bias=b_half[:, j:j + 1], scale=0.5)
+
+        def turn_back(j):
+            back[j] = ps_tp.tile([P, ROW_TILES, P], F32, name="back", tag="tp")
+            for i in range(ROW_TILES):
+                nc.tensor.transpose(back[j][:, i, :], gate_t[j][:, i * P:(i + 1) * P], ident[:])
+
+        def fin(j):
+            k, jj = divmod(j, 2)
+            nc.vector.scalar_tensor_tensor(
+                out=o_sb[k][:, :, jj * P:(jj + 1) * P],
+                in0=back[j][:],
+                scalar=1.0,
+                in1=ratio[k][:, :, jj * P:(jj + 1) * P],
+                op0=ALU.add,
+                op1=ALU.mult,
+            )
+
+        out_view = out.rearrange("(i p) d -> p i d", p=P)
+
+        def store(k):
+            nc.sync.dma_start(out=out_view[:, :, k * CHUNK:(k + 1) * CHUNK], in_=o_sb[k][:])
+
+        def store_tile(j):
+            k, jj = divmod(j, 2)
+            nc.sync.dma_start(out=out_view[:, :, j * P:(j + 1) * P], in_=o_sb[k][:, :, jj * P:(jj + 1) * P])
+
+        def ln(rp):
+            nc.scalar.activation(
+                out=log_n[:, 2 * rp:2 * rp + 2, :],
+                in_=act_sb["n"][:, 2 * rp:2 * rp + 2, :],
+                func=ACT.Ln,
+                bias=EPS,
+                scale=1.0,
+            )
+
+        def exp(k):
+            nc.scalar.activation(
+                out=ratio[k][:], in_=log_n[:, :, k * CHUNK:(k + 1) * CHUNK], func=ACT.Exp, scale=-1.0
+            )
+
+        def rmul(k):
+            nc.vector.scalar_tensor_tensor(
+                out=ratio[k][:],
+                in0=act_sb["c"][:, :, k * CHUNK:(k + 1) * CHUNK],
+                scalar=0.5,
+                in1=ratio[k][:],
+                op0=ALU.mult,
+                op1=ALU.mult,
+            )
+
+        uint_g(0, 0)
+        uint_g(1, 0)
+        widen(0, 0, CHUNK)
+        wint(0)
+        uint_g(0, 1)
+        widen(0, CHUNK, CHUNK)
+        uint_g(1, 1)
+        wint(1)
+        quant_w(0)
+        order = (("x", 0, 0), ("x", 1, 0), ("x", 0, 1), ("x", 1, 1), ("h", 0, 0), ("h", 1, 0), ("h", 0, 1), ("h", 1, 1))
+        for s in range(0, 8, 2):
+            turn_act(*order[s])
+            turn_act(*order[s + 1])
+            copy_act(*order[s], XCOPY[s])
+            copy_act(*order[s + 1], XCOPY[s + 1])
+            if s == 2:
+                quant_w(1)
+        widen(1, 0, HALF)
+        quant_x(0)
+        uint(2)
+        quant_x(1)
+        uint(3)
+        mx(0)
+        mx(1)
+        mx(2)
+        mx(3)
+        wint(2)
+        ln(0)
+        ln(1)
+        wint(3)
+        quant_w(2)
+        exp(0)
+        exp(1)
+        quant_w(3)
+        rmul(0)
+        rmul(1)
+        for j in range(8):
+            tanh(j)
+            turn_back(j)
+            if j + 4 < 8:
+                mx(j + 4)
+            if j in (1, 3):
+                exp(j // 2 + 2)
+            fin(j)
+            if j in (1, 3):
+                rmul(j // 2 + 2)
+            if j in (1, 3, 5):
+                store(j // 2)
+            if j in (6, 7):
+                store_tile(j)

@@ -17,14 +17,25 @@ ALU = mybir.AluOpType
 
 P = 128
 PACK = 4
-K_PASS = P * PACK
 ROW_TILES = B // P
+CH_TILES = D_H // P
 CHUNK = 256
-N_CHUNKS = D_H // CHUNK
 HALF = 512
 EPS = 1e-6
 
-XCOPY = ("s", "s", "s", "s", "v", "v", "v", "v")
+ORDER = (
+    "Lw1", "wd13", "wd10", "wd11", "Lw02", "Lw03", "Lw01", "Lw00", "Lx1", "wd12", "Lx0", "Tx11", "wd01",
+    "wd03", "wd02", "Lh1", "Tx01", "wi11", "Lh0", "wd00", "wi10", "Tx00", "Tx10", "wi00", "wi01", "Ln0",
+    "Lu10", "Th00", "Th01", "xcx11", "q10", "q00", "Lu00", "xcx10", "xcx01", "q11", "Ln1", "Th10", "q01",
+    "xcx00", "qxx", "ln0", "Th11", "mx10", "mx00", "xch00", "xch01", "xch11", "ui10", "xch10", "ui00", "q30",
+    "mx11", "Lu11", "Lu01", "qxh", "Lc1", "mx30", "ln1", "q20", "ex0", "mx20", "ui11", "ui01", "Lc0", "mx01",
+    "ex1", "th2", "th0", "q31", "mx31", "q21", "rm1", "rm0", "bk2", "th1", "mx21", "ex3", "fi2", "rm3",
+    "th3", "bk3", "ex2", "fi3", "bk0", "bk1", "th4", "th6", "fi0", "bk4", "fi1", "th5", "st1", "bk6", "th7",
+    "rm2", "fi6", "bk7", "st0", "bk5", "fi7", "sj6", "sj7", "fi5", "fi4", "st2",
+)
+ON_VECTOR = (
+    "wd02", "wd03", "wi00", "ui00", "ui01", "wd10", "wd11", "wi10", "ui10", "wi11", "ui11", "xcx01",
+)
 
 
 def tile_slstmcell_pb_kernel(tc, x, h_prev, c, n, W_o_bytes, W_o_scale, b_o, U_o, out):
@@ -32,114 +43,97 @@ def tile_slstmcell_pb_kernel(tc, x, h_prev, c, n, W_o_bytes, W_o_scale, b_o, U_o
     with ExitStack() as ctx:
         keep = ctx.enter_context(tc.tile_pool(name="keep", bufs=1))
         rot = ctx.enter_context(tc.tile_pool(name="rot", bufs=3))
-        ps_acc = ctx.enter_context(tc.psum_pool(name="ps_acc", bufs=4))
-        ps_tp = ctx.enter_context(tc.psum_pool(name="ps_tp", bufs=4))
+        psum = ctx.enter_context(tc.psum_pool(name="psum", bufs=8))
         ctx.enter_context(tc.manual_schedule())
 
+        wsc = keep.tile([P, 2, PACK], F32, name="wsc")
+        nc.scalar.dma_start(out=wsc[:], in_=W_o_scale.rearrange("(g p t) o -> p g (t o)", p=P, t=PACK))
+        b_rows = keep.tile([P, P], BF16, name="b_rows")
+        nc.gpsimd.memset(b_rows[:], 0.0)
+        nc.scalar.dma_start(out=b_rows[0:CH_TILES, :], in_=b_o.rearrange("(j p) -> j p", p=P))
         one = keep.tile([P, 1], F32, name="one")
         nc.gpsimd.memset(one[:], 1.0)
         scratch = keep.tile([P, 1], F32, name="scratch")
-        wsc = keep.tile([P, 2, PACK], F32, name="wsc")
-        nc.sync.dma_start(out=wsc[:], in_=W_o_scale.rearrange("(g p t) o -> p g (t o)", p=P, t=PACK))
-        b_sb = keep.tile([P, D_H // P], BF16, name="b_sb")
         nc.scalar.activation(out=scratch[:], in_=one[:], func=ACT.Ln)
+        ident_b = keep.tile([P, P], BF16, name="ident_b")
+        make_identity(nc, ident_b[:])
         ident = keep.tile([P, P], F32, name="ident")
         make_identity(nc, ident[:])
-        b_half = keep.tile([P, D_H // P], F32, name="b_half")
+        b_cols = psum.tile([P, P], BF16, name="b_cols", tag="bank")
+        nc.tensor.transpose(b_cols[:], b_rows[:], ident_b[:])
+        b_half = keep.tile([P, CH_TILES], F32, name="b_half")
+        nc.vector.tensor_scalar(out=b_half[:], in0=b_cols[:, 0:CH_TILES], scalar1=0.5, scalar2=None, op0=ALU.mult)
 
         w_view = W_o_bytes.rearrange("(g p t) d -> g p t d", p=P, t=PACK)
         u_view = U_o.rearrange("(g p t) d -> g p t d", p=P, t=PACK)
-        w8 = [keep.tile([P, 2, PACK, HALF], U8, name="w8_%d" % hf) for hf in range(2)]
-        u_raw = [keep.tile([P, 2, PACK, HALF], BF16, name="u_raw_%d" % hf) for hf in range(2)]
+        out_view = out.rearrange("(p i) d -> p i d", i=ROW_TILES)
+        dram = {"x": x, "h": h_prev, "n": n, "c": c}
+        w8 = [keep.tile([P, PACK, D_H], U8, name="w8_%d" % g) for g in range(2)]
+        raw = [keep.tile([P, PACK, D_H], BF16, name="raw_%d" % q) for q in range(4)]
         act_sb = {}
         for name in ("x", "h", "n", "c"):
             act_sb[name] = keep.tile([P, ROW_TILES, D_IN], BF16, name="%s_sb" % name)
-
-        def load_w(g, hf):
-            nc.sync.dma_start(out=w8[hf][:, g, :, :], in_=w_view[g][:, :, hf * HALF:(hf + 1) * HALF])
-
-        def load_u(g, hf):
-            nc.sync.dma_start(out=u_raw[hf][:, g, :, :], in_=u_view[g][:, :, hf * HALF:(hf + 1) * HALF])
-
-        def load_act(name, src, rp):
-            nc.sync.dma_start(
-                out=act_sb[name][:, 2 * rp:2 * rp + 2, :],
-                in_=src.rearrange("(i p) k -> p i k", p=P)[:, 2 * rp:2 * rp + 2, :],
-            )
-
-        load_w(0, 0)
-        load_u(0, 0)
-        load_w(1, 0)
-        load_u(1, 0)
-        load_act("x", x, 0)
-        load_act("x", x, 1)
-        load_act("h", h_prev, 0)
-        load_act("h", h_prev, 1)
-        load_w(0, 1)
-        load_w(1, 1)
-        load_u(0, 1)
-        load_u(1, 1)
-        with nc.allow_non_contiguous_dma(reason="bias: one element a partition, 1024 elements in all"):
-            nc.sync.dma_start(out=b_sb[:], in_=b_o.rearrange("(j p) -> p j", p=P))
-        nc.gpsimd.tensor_scalar(out=b_half[:], in0=b_sb[:], scalar1=0.5, scalar2=0.0, op0=ALU.mult, op1=ALU.add)
-        load_act("n", n, 0)
-        load_act("n", n, 1)
-        load_act("c", c, 0)
-        load_act("c", c, 1)
-
-        w_wide = [keep.tile([P, 2, PACK, HALF], BF16, name="w_wide_%d" % hf) for hf in range(2)]
-        wg = [keep.tile([P, 4, CHUNK, PACK], BF16, name="wg_%d" % k, align_bytes=64) for k in range(N_CHUNKS)]
-        wq = [keep.tile([P, 4 * CHUNK], U32, name="wq_%d" % k, align_bytes=64) for k in range(N_CHUNKS)]
-        ws = [keep.tile([P, 4 * CHUNK], U8, name="ws_%d" % k, align_bytes=64) for k in range(N_CHUNKS)]
+        wg = [keep.tile([P, D_H, PACK], BF16, name="wg_%d" % q, align_bytes=64) for q in range(4)]
+        wq = [keep.tile([P, D_H], U32, name="wq_%d" % q, align_bytes=64) for q in range(4)]
+        ws = [keep.tile([P, D_H], U8, name="ws_%d" % q, align_bytes=64) for q in range(4)]
         xg = [keep.tile([P, 2 * B * PACK], BF16, name="xg_%d" % a, align_bytes=64) for a in range(2)]
         xq = [keep.tile([P, 2 * B], U32, name="xq_%d" % a, align_bytes=64) for a in range(2)]
         xs = [keep.tile([P, 2 * B], U8, name="xs_%d" % a, align_bytes=64) for a in range(2)]
         log_n = keep.tile([P, ROW_TILES, D_H], F32, name="log_n")
-        ratio = [keep.tile([P, ROW_TILES, CHUNK], F32, name="ratio_%d" % k) for k in range(N_CHUNKS)]
-        o_sb = [keep.tile([P, ROW_TILES, CHUNK], F32, name="o_sb_%d" % k) for k in range(N_CHUNKS)]
-
-        def widen(hf, c0, width):
-            for g in range(2):
-                for t in range(PACK):
-                    nc.scalar.activation(
-                        out=w_wide[hf][:, g, t, c0:c0 + width],
-                        in_=w8[hf][:, g, t, c0:c0 + width].bitcast(FP8),
-                        func=ACT.Copy,
-                        scale=wsc[:, g, t:t + 1],
-                    )
-
-        def wint(k):
-            hf, c0 = divmod(k * CHUNK, HALF)
-            nc.vector.tensor_copy(
-                out=wg[k][:, 0:2, :, :],
-                in_=w_wide[hf][:, :, :, c0:c0 + CHUNK].rearrange("p g t d -> p g d t"),
-            )
-
-        def uint_g(k, g):
-            hf, c0 = divmod(k * CHUNK, HALF)
-            nc.vector.tensor_copy(
-                out=wg[k][:, 2 + g, :, :],
-                in_=u_raw[hf][:, g, :, c0:c0 + CHUNK].rearrange("p t d -> p d t"),
-            )
-
-        def uint(k):
-            hf, c0 = divmod(k * CHUNK, HALF)
-            nc.vector.tensor_copy(
-                out=wg[k][:, 2:4, :, :],
-                in_=u_raw[hf][:, :, :, c0:c0 + CHUNK].rearrange("p g t d -> p g d t"),
-            )
-
-        def quant_w(k):
-            nc.vector.quantize_mx(
-                out=wq[k][:].bitcast(FP8X4),
-                scales=ws[k][:],
-                in_=wg[k][:].rearrange("p q d t -> p (q d t)"),
-            )
-
+        ratio = [keep.tile([P, ROW_TILES, CHUNK], F32, name="ratio_%d" % k) for k in range(4)]
+        o_sb = [keep.tile([P, ROW_TILES, CHUNK], F32, name="o_sb_%d" % k) for k in range(4)]
         banks = {}
+        acc = {}
+        passes_done = {}
+        gate_t = {}
+        back = {}
+
+        def load(s):
+            if s[0] == "w" and len(s) == 3:
+                g, t = int(s[1]), int(s[2])
+                nc.sync.dma_start(out=w8[g][:, t, :], in_=w_view[g][:, t, :])
+            elif s[0] == "w":
+                g = int(s[1])
+                nc.sync.dma_start(out=w8[g][:], in_=w_view[g])
+            elif s[0] == "u":
+                g, hf = int(s[1]), int(s[2])
+                cols = slice(hf * HALF, (hf + 1) * HALF)
+                nc.sync.dma_start(out=raw[2 + g][:, :, cols], in_=u_view[g][:, :, cols])
+            else:
+                rp = int(s[1])
+                rows = slice(2 * rp, 2 * rp + 2)
+                nc.sync.dma_start(
+                    out=act_sb[s[0]][:, rows, :],
+                    in_=dram[s[0]].rearrange("(p i) k -> p i k", i=ROW_TILES)[:, rows, :],
+                )
+
+        def widen(g, t, on_vector):
+            src = w8[g][:, t, :].bitcast(FP8)
+            if on_vector:
+                nc.vector.tensor_scalar(
+                    out=raw[g][:, t, :], in0=src, scalar1=wsc[:, g, t:t + 1], scalar2=None, op0=ALU.mult
+                )
+            else:
+                nc.scalar.activation(out=raw[g][:, t, :], in_=src, func=ACT.Copy, scale=wsc[:, g, t:t + 1])
+
+        def interleave(q, hf, on_vector):
+            cols = slice(hf * HALF, (hf + 1) * HALF)
+            src = raw[q][:, :, cols].rearrange("p t d -> p d t")
+            if on_vector:
+                nc.vector.tensor_copy(out=wg[q][:, cols, :], in_=src)
+            else:
+                nc.scalar.copy(out=wg[q][:, cols, :], in_=src)
+
+        def quant_w(q, hf):
+            cols = slice(hf * HALF, (hf + 1) * HALF)
+            nc.vector.quantize_mx(
+                out=wq[q][:, cols].bitcast(FP8X4),
+                scales=ws[q][:, cols],
+                in_=wg[q][:, cols, :].rearrange("p d t -> p (d t)"),
+            )
 
         def turn_act(name, g, rp):
-            bank = ps_tp.tile([P, 2, 2 * P], F32, name="bank", tag="tp")
+            bank = psum.tile([P, 2, 2 * P], F32, name="bank", tag="bank")
             banks[(name, g, rp)] = bank
             for ii in range(2):
                 words = act_sb[name][:, 2 * rp + ii, :].bitcast(F32)
@@ -150,44 +144,43 @@ def tile_slstmcell_pb_kernel(tc, x, h_prev, c, n, W_o_bytes, W_o_scale, b_o, U_o
                         ident[:],
                     )
 
-        def copy_act(name, g, rp, engine):
+        def copy_act(name, g, rp, on_vector):
             a = 0 if name == "x" else 1
             r0 = g * B + rp * 2 * P
             dst = xg[a][:].bitcast(F32).rearrange("p (r u) -> p r u", u=2)[:, r0:r0 + 2 * P, :]
             src = banks[(name, g, rp)][:].rearrange("p u r -> p r u")
-            if engine == "s":
-                nc.scalar.copy(out=dst, in_=src)
-            else:
+            if on_vector:
                 nc.vector.tensor_copy(out=dst, in_=src)
+            else:
+                nc.scalar.copy(out=dst, in_=src)
 
         def quant_x(a):
             nc.vector.quantize_mx(out=xq[a][:].bitcast(FP8X4), scales=xs[a][:], in_=xg[a][:])
 
-        acc = {}
-        gate_t = {}
-        back = {}
-
-        def mx(j):
-            k, jj = divmod(j, 2)
-            acc[j] = ps_acc.tile([P, B], F32, name="acc", tag="acc")
-            for q in range(4):
-                cols = slice(q * CHUNK + jj * P, q * CHUNK + (jj + 1) * P)
+        def mx(q, hh):
+            for j in range(4 * hh, 4 * hh + 4):
+                if j not in acc:
+                    acc[j] = psum.tile([P, B], F32, name="acc", tag="bank")
+                    passes_done[j] = 0
+                cols = slice(j * P, (j + 1) * P)
+                toks = slice((q % 2) * B, (q % 2 + 1) * B)
                 nc.tensor.matmul_mx(
                     out=acc[j][:],
-                    lhsT=wq[k][:, cols].bitcast(FP8X4),
-                    lhsT_scale=ws[k][:, cols],
-                    rhs=xq[q // 2][:, (q % 2) * B:(q % 2 + 1) * B].bitcast(FP8X4),
-                    rhs_scale=xs[q // 2][:, (q % 2) * B:(q % 2 + 1) * B],
-                    start=(q == 0),
-                    stop=(q == 3),
+                    lhsT=wq[q][:, cols].bitcast(FP8X4),
+                    lhsT_scale=ws[q][:, cols],
+                    rhs=xq[q // 2][:, toks].bitcast(FP8X4),
+                    rhs_scale=xs[q // 2][:, toks],
+                    start=(passes_done[j] == 0),
+                    stop=(passes_done[j] == 3),
                 )
+                passes_done[j] += 1
 
         def tanh(j):
             gate_t[j] = rot.tile([P, B], F32, name="gate_t", tag="gate_t")
             nc.scalar.activation(out=gate_t[j][:], in_=acc[j][:], func=ACT.Tanh, bias=b_half[:, j:j + 1], scale=0.5)
 
         def turn_back(j):
-            back[j] = ps_tp.tile([P, ROW_TILES, P], F32, name="back", tag="tp")
+            back[j] = psum.tile([P, ROW_TILES, P], F32, name="back", tag="bank")
             for i in range(ROW_TILES):
                 nc.tensor.transpose(back[j][:, i, :], gate_t[j][:, i * P:(i + 1) * P], ident[:])
 
@@ -202,8 +195,6 @@ def tile_slstmcell_pb_kernel(tc, x, h_prev, c, n, W_o_bytes, W_o_scale, b_o, U_o
                 op1=ALU.mult,
             )
 
-        out_view = out.rearrange("(i p) d -> p i d", p=P)
-
         def store(k):
             nc.sync.dma_start(out=out_view[:, :, k * CHUNK:(k + 1) * CHUNK], in_=o_sb[k][:])
 
@@ -212,13 +203,8 @@ def tile_slstmcell_pb_kernel(tc, x, h_prev, c, n, W_o_bytes, W_o_scale, b_o, U_o
             nc.sync.dma_start(out=out_view[:, :, j * P:(j + 1) * P], in_=o_sb[k][:, :, jj * P:(jj + 1) * P])
 
         def ln(rp):
-            nc.scalar.activation(
-                out=log_n[:, 2 * rp:2 * rp + 2, :],
-                in_=act_sb["n"][:, 2 * rp:2 * rp + 2, :],
-                func=ACT.Ln,
-                bias=EPS,
-                scale=1.0,
-            )
+            rows = slice(2 * rp, 2 * rp + 2)
+            nc.scalar.activation(out=log_n[:, rows, :], in_=act_sb["n"][:, rows, :], func=ACT.Ln, bias=EPS, scale=1.0)
 
         def exp(k):
             nc.scalar.activation(
@@ -235,53 +221,41 @@ def tile_slstmcell_pb_kernel(tc, x, h_prev, c, n, W_o_bytes, W_o_scale, b_o, U_o
                 op1=ALU.mult,
             )
 
-        uint_g(0, 0)
-        uint_g(1, 0)
-        widen(0, 0, CHUNK)
-        wint(0)
-        uint_g(0, 1)
-        widen(0, CHUNK, CHUNK)
-        uint_g(1, 1)
-        wint(1)
-        quant_w(0)
-        order = (("x", 0, 0), ("x", 1, 0), ("x", 0, 1), ("x", 1, 1), ("h", 0, 0), ("h", 1, 0), ("h", 0, 1), ("h", 1, 1))
-        for s in range(0, 8, 2):
-            turn_act(*order[s])
-            turn_act(*order[s + 1])
-            copy_act(*order[s], XCOPY[s])
-            copy_act(*order[s + 1], XCOPY[s + 1])
-            if s == 2:
-                quant_w(1)
-        widen(1, 0, HALF)
-        quant_x(0)
-        uint(2)
-        quant_x(1)
-        uint(3)
-        mx(0)
-        mx(1)
-        mx(2)
-        mx(3)
-        wint(2)
-        ln(0)
-        ln(1)
-        wint(3)
-        quant_w(2)
-        exp(0)
-        exp(1)
-        quant_w(3)
-        rmul(0)
-        rmul(1)
-        for j in range(8):
-            tanh(j)
-            turn_back(j)
-            if j + 4 < 8:
-                mx(j + 4)
-            if j in (1, 3):
-                exp(j // 2 + 2)
-            fin(j)
-            if j in (1, 3):
-                rmul(j // 2 + 2)
-            if j in (1, 3, 5):
-                store(j // 2)
-            if j in (6, 7):
-                store_tile(j)
+        for s in ORDER:
+            v = s in ON_VECTOR
+            if s[0] == "L":
+                load(s[1:])
+            elif s[:2] == "wd":
+                widen(int(s[2]), int(s[3]), v)
+            elif s[:2] == "wi":
+                interleave(int(s[2]), int(s[3]), v)
+            elif s[:2] == "ui":
+                interleave(2 + int(s[2]), int(s[3]), v)
+            elif s[:2] == "qx":
+                quant_x(0 if s[2] == "x" else 1)
+            elif s[0] == "q":
+                quant_w(int(s[1]), int(s[2]))
+            elif s[0] == "T":
+                turn_act(s[1], int(s[2]), int(s[3]))
+            elif s[:2] == "xc":
+                copy_act(s[2], int(s[3]), int(s[4]), v)
+            elif s[:2] == "mx":
+                mx(int(s[2]), int(s[3]))
+            elif s[:2] == "ln":
+                ln(int(s[2]))
+            elif s[:2] == "ex":
+                exp(int(s[2]))
+            elif s[:2] == "rm":
+                rmul(int(s[2]))
+            elif s[:2] == "th":
+                tanh(int(s[2]))
+            elif s[:2] == "bk":
+                turn_back(int(s[2]))
+            elif s[:2] == "fi":
+                fin(int(s[2]))
+            elif s[:2] == "st":
+                store(int(s[2]))
+            elif s[:2] == "sj":
+                store_tile(int(s[2]))
+            else:
+                raise ValueError(s)

@@ -23,20 +23,6 @@ CHUNK = 256
 HALF = 512
 EPS = 1e-6
 
-ORDER = (
-    "Lw1", "wd13", "wd10", "wd11", "Lw02", "Lw03", "Lw01", "Lw00", "Lx1", "wd12", "Lx0", "Tx11", "wd01",
-    "wd03", "wd02", "Lh1", "Tx01", "wi11", "Lh0", "wd00", "wi10", "Tx00", "Tx10", "wi00", "wi01", "Ln0",
-    "Lu10", "Th00", "Th01", "xcx11", "q10", "q00", "Lu00", "xcx10", "xcx01", "q11", "Ln1", "Th10", "q01",
-    "xcx00", "qxx", "ln0", "Th11", "mx10", "mx00", "xch00", "xch01", "xch11", "ui10", "xch10", "ui00", "q30",
-    "mx11", "Lu11", "Lu01", "qxh", "Lc1", "mx30", "ln1", "q20", "ex0", "mx20", "ui11", "ui01", "Lc0", "mx01",
-    "ex1", "th2", "th0", "q31", "mx31", "q21", "rm1", "rm0", "bk2", "th1", "mx21", "ex3", "fi2", "rm3",
-    "th3", "bk3", "ex2", "fi3", "bk0", "bk1", "th4", "th6", "fi0", "bk4", "fi1", "th5", "st1", "bk6", "th7",
-    "rm2", "fi6", "bk7", "st0", "bk5", "fi7", "sj6", "sj7", "fi5", "fi4", "st2",
-)
-ON_VECTOR = (
-    "wd02", "wd03", "wi00", "ui00", "ui01", "wd10", "wd11", "wi10", "ui10", "wi11", "ui11", "xcx01",
-)
-
 
 def tile_slstmcell_pb_kernel(tc, x, h_prev, c, n, W_o_bytes, W_o_scale, b_o, U_o, out):
     nc = tc.nc
@@ -76,53 +62,58 @@ def tile_slstmcell_pb_kernel(tc, x, h_prev, c, n, W_o_bytes, W_o_scale, b_o, U_o
         wg = [keep.tile([P, D_H, PACK], BF16, name="wg_%d" % q, align_bytes=64) for q in range(4)]
         wq = [keep.tile([P, D_H], U32, name="wq_%d" % q, align_bytes=64) for q in range(4)]
         ws = [keep.tile([P, D_H], U8, name="ws_%d" % q, align_bytes=64) for q in range(4)]
-        xg = [keep.tile([P, 2 * B * PACK], BF16, name="xg_%d" % a, align_bytes=64) for a in range(2)]
-        xq = [keep.tile([P, 2 * B], U32, name="xq_%d" % a, align_bytes=64) for a in range(2)]
-        xs = [keep.tile([P, 2 * B], U8, name="xs_%d" % a, align_bytes=64) for a in range(2)]
+        xg = {}
+        xq = {}
+        xs = {}
+        for name in ("x", "h"):
+            xg[name] = keep.tile([P, 2 * B * PACK], BF16, name="xg_%s" % name, align_bytes=64)
+            xq[name] = keep.tile([P, 2 * B], U32, name="xq_%s" % name, align_bytes=64)
+            xs[name] = keep.tile([P, 2 * B], U8, name="xs_%s" % name, align_bytes=64)
         log_n = keep.tile([P, ROW_TILES, D_H], F32, name="log_n")
         ratio = [keep.tile([P, ROW_TILES, CHUNK], F32, name="ratio_%d" % k) for k in range(4)]
         o_sb = [keep.tile([P, ROW_TILES, CHUNK], F32, name="o_sb_%d" % k) for k in range(4)]
         banks = {}
         acc = {}
-        passes_done = {}
         gate_t = {}
         back = {}
 
-        def load(s):
-            if s[0] == "w" and len(s) == 3:
-                g, t = int(s[1]), int(s[2])
-                nc.sync.dma_start(out=w8[g][:, t, :], in_=w_view[g][:, t, :])
-            elif s[0] == "w":
-                g = int(s[1])
-                nc.sync.dma_start(out=w8[g][:], in_=w_view[g])
-            elif s[0] == "u":
-                g, hf = int(s[1]), int(s[2])
-                cols = slice(hf * HALF, (hf + 1) * HALF)
-                nc.sync.dma_start(out=raw[2 + g][:, :, cols], in_=u_view[g][:, :, cols])
-            else:
-                rp = int(s[1])
-                rows = slice(2 * rp, 2 * rp + 2)
-                nc.sync.dma_start(
-                    out=act_sb[s[0]][:, rows, :],
-                    in_=dram[s[0]].rearrange("(p i) k -> p i k", i=ROW_TILES)[:, rows, :],
-                )
+        def load_w_plane(g, t):
+            nc.sync.dma_start(out=w8[g][:, t, :], in_=w_view[g][:, t, :])
 
-        def widen(g, t, on_vector):
-            src = w8[g][:, t, :].bitcast(FP8)
-            if on_vector:
-                nc.vector.tensor_scalar(
-                    out=raw[g][:, t, :], in0=src, scalar1=wsc[:, g, t:t + 1], scalar2=None, op0=ALU.mult
-                )
-            else:
-                nc.scalar.activation(out=raw[g][:, t, :], in_=src, func=ACT.Copy, scale=wsc[:, g, t:t + 1])
+        def load_w(g):
+            nc.sync.dma_start(out=w8[g][:], in_=w_view[g])
 
-        def interleave(q, hf, on_vector):
+        def load_u(g, hf):
             cols = slice(hf * HALF, (hf + 1) * HALF)
-            src = raw[q][:, :, cols].rearrange("p t d -> p d t")
-            if on_vector:
-                nc.vector.tensor_copy(out=wg[q][:, cols, :], in_=src)
-            else:
-                nc.scalar.copy(out=wg[q][:, cols, :], in_=src)
+            nc.sync.dma_start(out=raw[2 + g][:, :, cols], in_=u_view[g][:, :, cols])
+
+        def load_act(name, rp):
+            rows = slice(2 * rp, 2 * rp + 2)
+            nc.sync.dma_start(
+                out=act_sb[name][:, rows, :],
+                in_=dram[name].rearrange("(p i) k -> p i k", i=ROW_TILES)[:, rows, :],
+            )
+
+        def widen_s(g, t):
+            nc.scalar.activation(
+                out=raw[g][:, t, :], in_=w8[g][:, t, :].bitcast(FP8), func=ACT.Copy, scale=wsc[:, g, t:t + 1]
+            )
+
+        def widen_v(g, t):
+            nc.vector.tensor_scalar(
+                out=raw[g][:, t, :],
+                in0=w8[g][:, t, :].bitcast(FP8),
+                scalar1=wsc[:, g, t:t + 1],
+                scalar2=None,
+                op0=ALU.mult,
+            )
+
+        def interleave(q, hf, copy):
+            cols = slice(hf * HALF, (hf + 1) * HALF)
+            copy(
+                out=wg[q][:, cols, :].rearrange("p (e i) t -> p e t i", i=4),
+                in_=raw[q][:, :, cols].rearrange("p t (e i) -> p e t i", i=4),
+            )
 
         def quant_w(q, hf):
             cols = slice(hf * HALF, (hf + 1) * HALF)
@@ -144,36 +135,32 @@ def tile_slstmcell_pb_kernel(tc, x, h_prev, c, n, W_o_bytes, W_o_scale, b_o, U_o
                         ident[:],
                     )
 
-        def copy_act(name, g, rp, on_vector):
-            a = 0 if name == "x" else 1
+        def copy_act(name, g, rp):
             r0 = g * B + rp * 2 * P
-            dst = xg[a][:].bitcast(F32).rearrange("p (r u) -> p r u", u=2)[:, r0:r0 + 2 * P, :]
-            src = banks[(name, g, rp)][:].rearrange("p u r -> p r u")
-            if on_vector:
-                nc.vector.tensor_copy(out=dst, in_=src)
-            else:
-                nc.scalar.copy(out=dst, in_=src)
+            nc.scalar.copy(
+                out=xg[name][:].bitcast(F32).rearrange("p (r u) -> p r u", u=2)[:, r0:r0 + 2 * P, :],
+                in_=banks[(name, g, rp)][:].rearrange("p u r -> p r u"),
+            )
 
-        def quant_x(a):
-            nc.vector.quantize_mx(out=xq[a][:].bitcast(FP8X4), scales=xs[a][:], in_=xg[a][:])
+        def quant_x(name):
+            nc.vector.quantize_mx(out=xq[name][:].bitcast(FP8X4), scales=xs[name][:], in_=xg[name][:])
 
-        def mx(q, hh):
-            for j in range(4 * hh, 4 * hh + 4):
-                if j not in acc:
+        def mx(q, hf, first, last):
+            name = "x" if q < 2 else "h"
+            toks = slice((q % 2) * B, (q % 2 + 1) * B)
+            for j in range(4 * hf, 4 * hf + 4):
+                if first:
                     acc[j] = psum.tile([P, B], F32, name="acc", tag="bank")
-                    passes_done[j] = 0
                 cols = slice(j * P, (j + 1) * P)
-                toks = slice((q % 2) * B, (q % 2 + 1) * B)
                 nc.tensor.matmul_mx(
                     out=acc[j][:],
                     lhsT=wq[q][:, cols].bitcast(FP8X4),
                     lhsT_scale=ws[q][:, cols],
-                    rhs=xq[q // 2][:, toks].bitcast(FP8X4),
-                    rhs_scale=xs[q // 2][:, toks],
-                    start=(passes_done[j] == 0),
-                    stop=(passes_done[j] == 3),
+                    rhs=xq[name][:, toks].bitcast(FP8X4),
+                    rhs_scale=xs[name][:, toks],
+                    start=first,
+                    stop=last,
                 )
-                passes_done[j] += 1
 
         def tanh(j):
             gate_t[j] = rot.tile([P, B], F32, name="gate_t", tag="gate_t")
@@ -221,41 +208,79 @@ def tile_slstmcell_pb_kernel(tc, x, h_prev, c, n, W_o_bytes, W_o_scale, b_o, U_o
                 op1=ALU.mult,
             )
 
-        for s in ORDER:
-            v = s in ON_VECTOR
-            if s[0] == "L":
-                load(s[1:])
-            elif s[:2] == "wd":
-                widen(int(s[2]), int(s[3]), v)
-            elif s[:2] == "wi":
-                interleave(int(s[2]), int(s[3]), v)
-            elif s[:2] == "ui":
-                interleave(2 + int(s[2]), int(s[3]), v)
-            elif s[:2] == "qx":
-                quant_x(0 if s[2] == "x" else 1)
-            elif s[0] == "q":
-                quant_w(int(s[1]), int(s[2]))
-            elif s[0] == "T":
-                turn_act(s[1], int(s[2]), int(s[3]))
-            elif s[:2] == "xc":
-                copy_act(s[2], int(s[3]), int(s[4]), v)
-            elif s[:2] == "mx":
-                mx(int(s[2]), int(s[3]))
-            elif s[:2] == "ln":
-                ln(int(s[2]))
-            elif s[:2] == "ex":
-                exp(int(s[2]))
-            elif s[:2] == "rm":
-                rmul(int(s[2]))
-            elif s[:2] == "th":
-                tanh(int(s[2]))
-            elif s[:2] == "bk":
-                turn_back(int(s[2]))
-            elif s[:2] == "fi":
-                fin(int(s[2]))
-            elif s[:2] == "st":
-                store(int(s[2]))
-            elif s[:2] == "sj":
-                store_tile(int(s[2]))
-            else:
-                raise ValueError(s)
+        for t in (0, 2, 1, 3):
+            load_w_plane(0, t)
+        load_w(1)
+        for name in ("x", "h"):
+            for rp in range(2):
+                load_act(name, rp)
+        load_act("n", 0)
+        load_u(0, 0)
+        load_u(1, 0)
+        load_act("n", 1)
+        load_u(0, 1)
+        load_u(1, 1)
+        load_act("c", 0)
+        load_act("c", 1)
+
+        for g in range(2):
+            widen_s(g, 0)
+            widen_v(g, 2)
+            widen_s(g, 1)
+            widen_v(g, 3)
+        interleave(0, 0, nc.vector.tensor_copy)
+        interleave(0, 1, nc.vector.tensor_copy)
+        interleave(1, 0, nc.vector.tensor_copy)
+        interleave(1, 1, nc.scalar.copy)
+        for name in ("x", "h"):
+            for rp in range(2):
+                for g in range(2):
+                    turn_act(name, g, rp)
+        quant_w(0, 0)
+        quant_w(0, 1)
+        for rp in range(2):
+            for g in range(2):
+                copy_act("x", g, rp)
+        quant_w(1, 0)
+        quant_w(1, 1)
+        ln(0)
+        quant_x("x")
+        mx(0, 0, True, False)
+        mx(1, 0, False, False)
+        for rp in range(2):
+            for g in range(2):
+                copy_act("h", g, rp)
+        mx(0, 1, True, False)
+        mx(1, 1, False, False)
+        interleave(2, 0, nc.vector.tensor_copy)
+        interleave(3, 0, nc.vector.tensor_copy)
+        ln(1)
+        quant_w(2, 0)
+        quant_x("h")
+        quant_w(3, 0)
+        mx(2, 0, False, False)
+        mx(3, 0, False, True)
+        interleave(2, 1, nc.vector.tensor_copy)
+        interleave(3, 1, nc.vector.tensor_copy)
+        exp(0)
+        exp(1)
+        quant_w(2, 1)
+        quant_w(3, 1)
+        mx(2, 1, False, False)
+        mx(3, 1, False, True)
+        rmul(0)
+        rmul(1)
+        for j in range(CH_TILES):
+            tanh(j)
+            turn_back(j)
+            if j in (0, 2):
+                exp(j // 2 + 2)
+            fin(j)
+            if j == 0:
+                rmul(2)
+            if j in (1, 3, 5):
+                store(j // 2)
+            if j == 5:
+                rmul(3)
+            if j in (6, 7):
+                store_tile(j)

@@ -22,6 +22,7 @@ CH_TILES = D_H // P
 CHUNK = 256
 HALF = 512
 EPS = 1e-6
+LN2 = 0.6931471805599453
 
 
 def tile_slstmcell_pb_kernel(tc, x, h_prev, c, n, W_o_bytes, W_o_scale, b_o, U_o, out):
@@ -70,7 +71,7 @@ def tile_slstmcell_pb_kernel(tc, x, h_prev, c, n, W_o_bytes, W_o_scale, b_o, U_o
             xq[name] = keep.tile([P, 2 * B], U32, name="xq_%s" % name, align_bytes=64)
             xs[name] = keep.tile([P, 2 * B], U8, name="xs_%s" % name, align_bytes=64)
         log_n = keep.tile([P, ROW_TILES, D_H], F32, name="log_n")
-        ratio = [keep.tile([P, ROW_TILES, CHUNK], F32, name="ratio_%d" % k) for k in range(4)]
+        ratio = [keep.tile([P, ROW_TILES, CHUNK], F32, name="ratio_%d" % k) for k in range(5)]
         o_sb = [keep.tile([P, ROW_TILES, CHUNK], F32, name="o_sb_%d" % k) for k in range(4)]
         banks = {}
         acc = {}
@@ -110,10 +111,7 @@ def tile_slstmcell_pb_kernel(tc, x, h_prev, c, n, W_o_bytes, W_o_scale, b_o, U_o
 
         def interleave(q, hf, copy):
             cols = slice(hf * HALF, (hf + 1) * HALF)
-            copy(
-                out=wg[q][:, cols, :].rearrange("p (e i) t -> p e t i", i=4),
-                in_=raw[q][:, :, cols].rearrange("p t (e i) -> p e t i", i=4),
-            )
+            copy(out=wg[q][:, cols, :], in_=raw[q][:, :, cols].rearrange("p t d -> p d t"))
 
         def quant_w(q, hf):
             cols = slice(hf * HALF, (hf + 1) * HALF)
@@ -195,17 +193,12 @@ def tile_slstmcell_pb_kernel(tc, x, h_prev, c, n, W_o_bytes, W_o_scale, b_o, U_o
 
         def exp(k):
             nc.scalar.activation(
-                out=ratio[k][:], in_=log_n[:, :, k * CHUNK:(k + 1) * CHUNK], func=ACT.Exp, scale=-1.0
+                out=ratio[k + 1][:], in_=log_n[:, :, k * CHUNK:(k + 1) * CHUNK], func=ACT.Exp, bias=-LN2, scale=-1.0
             )
 
-        def rmul(k):
-            nc.vector.scalar_tensor_tensor(
-                out=ratio[k][:],
-                in0=act_sb["c"][:, :, k * CHUNK:(k + 1) * CHUNK],
-                scalar=0.5,
-                in1=ratio[k][:],
-                op0=ALU.mult,
-                op1=ALU.mult,
+        def rmul(k, engine):
+            engine.tensor_tensor(
+                out=ratio[k][:], in0=act_sb["c"][:, :, k * CHUNK:(k + 1) * CHUNK], in1=ratio[k + 1][:], op=ALU.mult
             )
 
         for t in (0, 2, 1, 3):
@@ -268,19 +261,16 @@ def tile_slstmcell_pb_kernel(tc, x, h_prev, c, n, W_o_bytes, W_o_scale, b_o, U_o
         quant_w(3, 1)
         mx(2, 1, False, False)
         mx(3, 1, False, True)
-        rmul(0)
-        rmul(1)
+        rmul(0, nc.vector)
+        rmul(1, nc.vector)
         for j in range(CH_TILES):
             tanh(j)
             turn_back(j)
             if j in (0, 2):
                 exp(j // 2 + 2)
+                rmul(j // 2 + 2, nc.gpsimd)
             fin(j)
-            if j == 0:
-                rmul(2)
             if j in (1, 3, 5):
                 store(j // 2)
-            if j == 5:
-                rmul(3)
             if j in (6, 7):
                 store_tile(j)

@@ -49,7 +49,6 @@ def tile_slstmcell_pb_kernel(tc, x, h_prev, c, n, W_o_bytes, W_o_scale, b_o, U_o
         b_cols = psum.tile([P, P], BF16, name="b_cols", tag="bank")
         nc.tensor.transpose(b_cols[:], b_rows[:], ident_b[:])
         b_half = keep.tile([P, CH_TILES], F32, name="b_half")
-        nc.vector.tensor_scalar(out=b_half[:], in0=b_cols[:, 0:CH_TILES], scalar1=0.5, scalar2=None, op0=ALU.mult)
 
         w_view = W_o_bytes.rearrange("(g p t) d -> g p t d", p=P, t=PACK)
         u_view = U_o.rearrange("(g p t) d -> g p t d", p=P, t=PACK)
@@ -88,8 +87,8 @@ def tile_slstmcell_pb_kernel(tc, x, h_prev, c, n, W_o_bytes, W_o_scale, b_o, U_o
             cols = slice(hf * HALF, (hf + 1) * HALF)
             nc.sync.dma_start(out=raw[2 + g][:, :, cols], in_=u_view[g][:, :, cols])
 
-        def load_act(name, rp):
-            rows = slice(2 * rp, 2 * rp + 2)
+        def load_act(name, i0, i1):
+            rows = slice(i0, i1)
             nc.sync.dma_start(
                 out=act_sb[name][:, rows, :],
                 in_=dram[name].rearrange("(p i) k -> p i k", i=ROW_TILES)[:, rows, :],
@@ -183,10 +182,6 @@ def tile_slstmcell_pb_kernel(tc, x, h_prev, c, n, W_o_bytes, W_o_scale, b_o, U_o
         def store(k):
             nc.sync.dma_start(out=out_view[:, :, k * CHUNK:(k + 1) * CHUNK], in_=o_sb[k][:])
 
-        def store_tile(j):
-            k, jj = divmod(j, 2)
-            nc.sync.dma_start(out=out_view[:, :, j * P:(j + 1) * P], in_=o_sb[k][:, :, jj * P:(jj + 1) * P])
-
         def ln(rp):
             rows = slice(2 * rp, 2 * rp + 2)
             nc.scalar.activation(out=log_n[:, rows, :], in_=act_sb["n"][:, rows, :], func=ACT.Ln, bias=EPS, scale=1.0)
@@ -205,16 +200,15 @@ def tile_slstmcell_pb_kernel(tc, x, h_prev, c, n, W_o_bytes, W_o_scale, b_o, U_o
             load_w_plane(0, t)
         load_w(1)
         for name in ("x", "h"):
-            for rp in range(2):
-                load_act(name, rp)
-        load_act("n", 0)
+            load_act(name, 0, 2)
+            load_act(name, 2, 4)
+        load_act("n", 0, 2)
         load_u(0, 0)
         load_u(1, 0)
-        load_act("n", 1)
+        load_act("n", 2, 4)
         load_u(0, 1)
         load_u(1, 1)
-        load_act("c", 0)
-        load_act("c", 1)
+        load_act("c", 0, 4)
 
         for g in range(2):
             widen_s(g, 0)
@@ -225,6 +219,7 @@ def tile_slstmcell_pb_kernel(tc, x, h_prev, c, n, W_o_bytes, W_o_scale, b_o, U_o
         interleave(0, 1, nc.vector.tensor_copy)
         interleave(1, 0, nc.vector.tensor_copy)
         interleave(1, 1, nc.scalar.copy)
+        nc.vector.tensor_scalar(out=b_half[:], in0=b_cols[:, 0:CH_TILES], scalar1=0.5, scalar2=None, op0=ALU.mult)
         for name in ("x", "h"):
             for rp in range(2):
                 for g in range(2):
@@ -270,7 +265,5 @@ def tile_slstmcell_pb_kernel(tc, x, h_prev, c, n, W_o_bytes, W_o_scale, b_o, U_o
                 exp(j // 2 + 2)
                 rmul(j // 2 + 2, nc.gpsimd)
             fin(j)
-            if j in (1, 3, 5):
+            if j % 2 == 1:
                 store(j // 2)
-            if j in (6, 7):
-                store_tile(j)

@@ -80,9 +80,6 @@ def tile_slstmcell_pb_kernel(tc, x, h_prev, c, n, W_o_bytes, W_o_scale, b_o, U_o
         def load_w_plane(g, t):
             nc.sync.dma_start(out=w8[g][:, t, :], in_=w_view[g][:, t, :])
 
-        def load_w(g):
-            nc.sync.dma_start(out=w8[g][:], in_=w_view[g])
-
         def load_u(g, hf):
             cols = slice(hf * HALF, (hf + 1) * HALF)
             nc.sync.dma_start(out=raw[2 + g][:, :, cols], in_=u_view[g][:, :, cols])
@@ -198,10 +195,10 @@ def tile_slstmcell_pb_kernel(tc, x, h_prev, c, n, W_o_bytes, W_o_scale, b_o, U_o
 
         for t in (0, 2, 1, 3):
             load_w_plane(0, t)
-        load_w(1)
+        for t in (0, 2, 1, 3):
+            load_w_plane(1, t)
         for name in ("x", "h"):
-            load_act(name, 0, 2)
-            load_act(name, 2, 4)
+            load_act(name, 0, 4)
         load_act("n", 0, 2)
         load_u(0, 0)
         load_u(1, 0)
@@ -258,12 +255,17 @@ def tile_slstmcell_pb_kernel(tc, x, h_prev, c, n, W_o_bytes, W_o_scale, b_o, U_o
         mx(3, 1, False, True)
         rmul(0, nc.vector)
         rmul(1, nc.vector)
-        for j in range(CH_TILES):
-            tanh(j)
-            turn_back(j)
-            if j in (0, 2):
-                exp(j // 2 + 2)
-                rmul(j // 2 + 2, nc.gpsimd)
-            fin(j)
-            if j % 2 == 1:
-                store(j // 2)
+        for k in range(4):
+            for j in (2 * k, 2 * k + 1):
+                tanh(j)
+                turn_back(j)
+            if k == 0:
+                exp(2)
+                rmul(2, nc.gpsimd)
+            if k == 2:
+                exp(3)
+            for j in (2 * k, 2 * k + 1):
+                fin(j)
+            store(k)
+            if k == 2:
+                rmul(3, nc.vector)

@@ -107,7 +107,10 @@ def tile_slstmcell_pb_kernel(tc, x, h_prev, c, n, W_o_bytes, W_o_scale, b_o, U_o
 
         def interleave(q, hf, copy):
             cols = slice(hf * HALF, (hf + 1) * HALF)
-            copy(out=wg[q][:, cols, :], in_=raw[q][:, :, cols].rearrange("p t d -> p d t"))
+            copy(
+                out=wg[q][:, cols, :].rearrange("p (c i) t -> p c t i", i=4),
+                in_=raw[q][:, :, cols].rearrange("p t (c i) -> p c t i", i=4),
+            )
 
         def quant_w(q, hf):
             cols = slice(hf * HALF, (hf + 1) * HALF)

@@ -55,11 +55,15 @@ def tile_slstmcell_pb_kernel(tc, x, h_prev, c, n, W_o_bytes, W_o_scale, b_o, U_o
         out_view = out.rearrange("(p i) d -> p i d", i=ROW_TILES)
         dram = {"x": x, "h": h_prev, "n": n, "c": c}
         w8 = [keep.tile([P, PACK, D_H], U8, name="w8_%d" % g) for g in range(2)]
-        raw = [keep.tile([P, PACK, D_H], BF16, name="raw_%d" % q) for q in range(4)]
+        raw = [keep.tile([P, PACK, D_H], BF16, name="raw_%d" % q) for q in range(2)]
+        raw_u = [[keep.tile([P, PACK, HALF], BF16, name="raw_u_%d_%d" % (g, hf)) for hf in range(2)] for g in range(2)]
         act_sb = {}
         for name in ("x", "h", "n", "c"):
             act_sb[name] = keep.tile([P, ROW_TILES, D_IN], BF16, name="%s_sb" % name)
-        wg = [keep.tile([P, D_H, PACK], BF16, name="wg_%d" % q, align_bytes=64) for q in range(4)]
+        wg = [
+            [keep.tile([P, HALF, PACK], BF16, name="wg_%d_%d" % (q, hf), align_bytes=64) for hf in range(2)]
+            for q in range(4)
+        ]
         wq = [keep.tile([P, D_H], U32, name="wq_%d" % q, align_bytes=64) for q in range(4)]
         ws = [keep.tile([P, D_H], U8, name="ws_%d" % q, align_bytes=64) for q in range(4)]
         xg = {}
@@ -82,7 +86,7 @@ def tile_slstmcell_pb_kernel(tc, x, h_prev, c, n, W_o_bytes, W_o_scale, b_o, U_o
 
         def load_u(g, hf):
             cols = slice(hf * HALF, (hf + 1) * HALF)
-            nc.sync.dma_start(out=raw[2 + g][:, :, cols], in_=u_view[g][:, :, cols])
+            nc.sync.dma_start(out=raw_u[g][hf][:], in_=u_view[g][:, :, cols])
 
         def load_act(name, i0, i1):
             rows = slice(i0, i1)
@@ -107,9 +111,10 @@ def tile_slstmcell_pb_kernel(tc, x, h_prev, c, n, W_o_bytes, W_o_scale, b_o, U_o
 
         def interleave(q, hf, copy):
             cols = slice(hf * HALF, (hf + 1) * HALF)
+            planes = raw[q][:, :, cols] if q < 2 else raw_u[q - 2][hf][:]
             copy(
-                out=wg[q][:, cols, :].rearrange("p (c i) t -> p c t i", i=4),
-                in_=raw[q][:, :, cols].rearrange("p t (c i) -> p c t i", i=4),
+                out=wg[q][hf][:].rearrange("p (c i) t -> p c t i", i=4),
+                in_=planes.rearrange("p t (c i) -> p c t i", i=4),
             )
 
         def quant_w(q, hf):
@@ -117,7 +122,7 @@ def tile_slstmcell_pb_kernel(tc, x, h_prev, c, n, W_o_bytes, W_o_scale, b_o, U_o
             nc.vector.quantize_mx(
                 out=wq[q][:, cols].bitcast(FP8X4),
                 scales=ws[q][:, cols],
-                in_=wg[q][:, cols, :].rearrange("p d t -> p (d t)"),
+                in_=wg[q][hf][:].rearrange("p d t -> p (d t)"),
             )
 
         def turn_act(name, g, rp):

@@ -21,6 +21,7 @@ ROW_TILES = B // P
 CH_TILES = D_H // P
 CHUNK = 256
 HALF = 512
+SHARE = 384
 EPS = 1e-6
 LN2 = 0.6931471805599453
 
@@ -109,12 +110,11 @@ def tile_slstmcell_pb_kernel(tc, x, h_prev, c, n, W_o_bytes, W_o_scale, b_o, U_o
                 op0=ALU.mult,
             )
 
-        def interleave(q, hf, copy):
-            cols = slice(hf * HALF, (hf + 1) * HALF)
-            planes = raw[q][:, :, cols] if q < 2 else raw_u[q - 2][hf][:]
+        def interleave(q, hf, copy, c0=0, c1=HALF):
+            planes = raw[q][:, :, hf * HALF:(hf + 1) * HALF] if q < 2 else raw_u[q - 2][hf][:]
             copy(
-                out=wg[q][hf][:].rearrange("p (c i) t -> p c t i", i=4),
-                in_=planes.rearrange("p t (c i) -> p c t i", i=4),
+                out=wg[q][hf][:, c0:c1, :].rearrange("p (c i) t -> p c t i", i=4),
+                in_=planes[:, :, c0:c1].rearrange("p t (c i) -> p c t i", i=4),
             )
 
         def quant_w(q, hf):
@@ -223,7 +223,8 @@ def tile_slstmcell_pb_kernel(tc, x, h_prev, c, n, W_o_bytes, W_o_scale, b_o, U_o
         interleave(0, 0, nc.vector.tensor_copy)
         interleave(0, 1, nc.vector.tensor_copy)
         interleave(1, 0, nc.vector.tensor_copy)
-        interleave(1, 1, nc.scalar.copy)
+        interleave(1, 1, nc.scalar.copy, 0, SHARE)
+        interleave(1, 1, nc.vector.tensor_copy, SHARE, HALF)
         nc.vector.tensor_scalar(out=b_half[:], in0=b_cols[:, 0:CH_TILES], scalar1=0.5, scalar2=None, op0=ALU.mult)
         for name in ("x", "h"):
             for rp in range(2):

@@ -21,7 +21,7 @@ ROW_TILES = B // P
 CH_TILES = D_H // P
 CHUNK = 256
 HALF = 512
-SHARE = 384
+SHARE = 128
 EPS = 1e-6
 LN2 = 0.6931471805599453
 
@@ -75,7 +75,8 @@ def tile_slstmcell_pb_kernel(tc, x, h_prev, c, n, W_o_bytes, W_o_scale, b_o, U_o
             xq[name] = keep.tile([P, 2 * B], U32, name="xq_%s" % name, align_bytes=64)
             xs[name] = keep.tile([P, 2 * B], U8, name="xs_%s" % name, align_bytes=64)
         log_n = keep.tile([P, ROW_TILES, D_H], F32, name="log_n")
-        ratio = [keep.tile([P, ROW_TILES, CHUNK], F32, name="ratio_%d" % k) for k in range(5)]
+        recip = [keep.tile([P, ROW_TILES, CHUNK], F32, name="recip_%d" % k) for k in range(4)]
+        ratio = [keep.tile([P, ROW_TILES, CHUNK], F32, name="ratio_%d" % k) for k in range(2)] + recip[0:2]
         o_sb = [keep.tile([P, ROW_TILES, CHUNK], F32, name="o_sb_%d" % k) for k in range(4)]
         banks = {}
         acc = {}
@@ -193,12 +194,21 @@ def tile_slstmcell_pb_kernel(tc, x, h_prev, c, n, W_o_bytes, W_o_scale, b_o, U_o
 
         def exp(k):
             nc.scalar.activation(
-                out=ratio[k + 1][:], in_=log_n[:, :, k * CHUNK:(k + 1) * CHUNK], func=ACT.Exp, bias=-LN2, scale=-1.0
+                out=recip[k][:], in_=log_n[:, :, k * CHUNK:(k + 1) * CHUNK], func=ACT.Exp, bias=-LN2, scale=-1.0
             )
 
         def rmul(k, engine):
             engine.tensor_tensor(
-                out=ratio[k][:], in0=act_sb["c"][:, :, k * CHUNK:(k + 1) * CHUNK], in1=ratio[k + 1][:], op=ALU.mult
+                out=ratio[k][:], in0=act_sb["c"][:, :, k * CHUNK:(k + 1) * CHUNK], in1=recip[k][:], op=ALU.mult
+            )
+
+        def rmul_tile(k, jj):
+            cols = slice(jj * P, (jj + 1) * P)
+            nc.gpsimd.tensor_tensor(
+                out=ratio[k][:, :, cols],
+                in0=act_sb["c"][:, :, (2 * k + jj) * P:(2 * k + jj + 1) * P],
+                in1=recip[k][:, :, cols],
+                op=ALU.mult,
             )
 
         for t in (0, 2, 1, 3):
@@ -268,13 +278,10 @@ def tile_slstmcell_pb_kernel(tc, x, h_prev, c, n, W_o_bytes, W_o_scale, b_o, U_o
             for j in (2 * k, 2 * k + 1):
                 tanh(j)
                 turn_back(j)
-            if k == 0:
-                exp(2)
-                rmul(2, nc.gpsimd)
-            if k == 2:
-                exp(3)
+            if k < 2:
+                exp(k + 2)
+                for jj in range(2):
+                    rmul_tile(k + 2, jj)
             for j in (2 * k, 2 * k + 1):
                 fin(j)
             store(k)
-            if k == 2:
-                rmul(3, nc.vector)

@@ -215,8 +215,9 @@ def tile_slstmcell_pb_kernel(tc, x, h_prev, c, n, W_o_bytes, W_o_scale, b_o, U_o
             load_w_plane(0, t)
         for t in (0, 2, 1, 3):
             load_w_plane(1, t)
-        for name in ("x", "h"):
-            load_act(name, 0, 4)
+        load_act("x", 0, 2)
+        load_act("x", 2, 4)
+        load_act("h", 0, 4)
         load_act("n", 0, 2)
         load_u(0, 0)
         load_u(1, 0)

@@ -21,7 +21,7 @@ ROW_TILES = B // P
 CH_TILES = D_H // P
 CHUNK = 256
 HALF = 512
-SHARE = 128
+SHARE = 384
 EPS = 1e-6
 LN2 = 0.6931471805599453
 
@@ -211,14 +211,14 @@ def tile_slstmcell_pb_kernel(tc, x, h_prev, c, n, W_o_bytes, W_o_scale, b_o, U_o
                 op=ALU.mult,
             )
 
-        for t in (0, 2, 1, 3):
+        for t in (2, 0, 3, 1):
             load_w_plane(0, t)
-        for t in (0, 2, 1, 3):
+        for t in (2, 3, 1, 0):
             load_w_plane(1, t)
         load_act("x", 0, 2)
         load_act("x", 2, 4)
-        load_act("h", 0, 4)
         load_act("n", 0, 2)
+        load_act("h", 0, 4)
         load_u(0, 0)
         load_u(1, 0)
         load_act("n", 2, 4)
@@ -226,11 +226,10 @@ def tile_slstmcell_pb_kernel(tc, x, h_prev, c, n, W_o_bytes, W_o_scale, b_o, U_o
         load_u(1, 1)
         load_act("c", 0, 4)
 
-        for g in range(2):
-            widen_s(g, 0)
-            widen_v(g, 2)
-            widen_s(g, 1)
-            widen_v(g, 3)
+        for g, t in ((0, 0), (0, 1), (1, 0)):
+            widen_s(g, t)
+        for g, t in ((0, 2), (0, 3), (1, 2), (1, 3), (1, 1)):
+            widen_v(g, t)
         interleave(0, 0, nc.vector.tensor_copy)
         interleave(0, 1, nc.vector.tensor_copy)
         interleave(1, 0, nc.vector.tensor_copy)

@@ -50,6 +50,8 @@ def tile_slstmcell_pb_kernel(tc, x, h_prev, c, n, W_o_bytes, W_o_scale, b_o, U_o
         b_cols = psum.tile([P, P], BF16, name="b_cols", tag="bank")
         nc.tensor.transpose(b_cols[:], b_rows[:], ident_b[:])
         b_half = keep.tile([P, CH_TILES], F32, name="b_half")
+        zeros = keep.tile([P, B], BF16, name="zeros")
+        nc.vector.memset(zeros[:], 0.0)
 
         w_view = W_o_bytes.rearrange("(g p t) d -> g p t d", p=P, t=PACK)
         u_view = U_o.rearrange("(g p t) d -> g p t d", p=P, t=PACK)
@@ -129,6 +131,8 @@ def tile_slstmcell_pb_kernel(tc, x, h_prev, c, n, W_o_bytes, W_o_scale, b_o, U_o
         def turn_act(name, g, rp):
             bank = psum.tile([P, 2, 2 * P], F32, name="bank", tag="bank")
             banks[(name, g, rp)] = bank
+            for i in range(5 if len(banks) == 1 else 1):
+                warm(bank)
             for ii in range(2):
                 words = act_sb[name][:, 2 * rp + ii, :].bitcast(F32)
                 for u in range(2):
@@ -137,6 +141,11 @@ def tile_slstmcell_pb_kernel(tc, x, h_prev, c, n, W_o_bytes, W_o_scale, b_o, U_o
                         words[:, 256 * g + u:256 * (g + 1):2],
                         ident[:],
                     )
+
+        def warm(bank):
+            nc.tensor.matmul(
+                bank[:].rearrange("p u r -> p (u r)"), lhsT=ident_b[:], rhs=zeros[:], start=True, stop=True
+            )
 
         def copy_act(name, g, rp):
             r0 = g * B + rp * 2 * P

@@ -50,8 +50,6 @@ def tile_slstmcell_pb_kernel(tc, x, h_prev, c, n, W_o_bytes, W_o_scale, b_o, U_o
         b_cols = psum.tile([P, P], BF16, name="b_cols", tag="bank")
         nc.tensor.transpose(b_cols[:], b_rows[:], ident_b[:])
         b_half = keep.tile([P, CH_TILES], F32, name="b_half")
-        zeros = keep.tile([P, B], BF16, name="zeros")
-        nc.vector.memset(zeros[:], 0.0)
 
         w_view = W_o_bytes.rearrange("(g p t) d -> g p t d", p=P, t=PACK)
         u_view = U_o.rearrange("(g p t) d -> g p t d", p=P, t=PACK)
@@ -131,8 +129,7 @@ def tile_slstmcell_pb_kernel(tc, x, h_prev, c, n, W_o_bytes, W_o_scale, b_o, U_o
         def turn_act(name, g, rp):
             bank = psum.tile([P, 2, 2 * P], F32, name="bank", tag="bank")
             banks[(name, g, rp)] = bank
-            for i in range(5 if len(banks) == 1 else 1):
-                warm(bank)
+            warm(bank[:, 0, 0:P], 6 if (g, rp) == (0, 0) else 1)
             for ii in range(2):
                 words = act_sb[name][:, 2 * rp + ii, :].bitcast(F32)
                 for u in range(2):
@@ -142,10 +139,9 @@ def tile_slstmcell_pb_kernel(tc, x, h_prev, c, n, W_o_bytes, W_o_scale, b_o, U_o
                         ident[:],
                     )
 
-        def warm(bank):
-            nc.tensor.matmul(
-                bank[:].rearrange("p u r -> p (u r)"), lhsT=ident_b[:], rhs=zeros[:], start=True, stop=True
-            )
+        def warm(out_cols, times):
+            for i in range(times):
+                nc.tensor.matmul(out_cols, lhsT=ident[:], rhs=ident[:], start=True, stop=True)
 
         def copy_act(name, g, rp):
             r0 = g * B + rp * 2 * P
@@ -180,6 +176,8 @@ def tile_slstmcell_pb_kernel(tc, x, h_prev, c, n, W_o_bytes, W_o_scale, b_o, U_o
 
         def turn_back(j):
             back[j] = psum.tile([P, ROW_TILES, P], F32, name="back", tag="bank")
+            if j in (4, 5):
+                warm(back[j][:, 0, :], 1)
             for i in range(ROW_TILES):
                 nc.tensor.transpose(back[j][:, i, :], gate_t[j][:, i * P:(i + 1) * P], ident[:])
 

from contextlib import ExitStack

import concourse.mybir as mybir
from concourse.masks import make_identity

B, D_IN, D_H = 512, 1024, 1024
FLOPS = 2 * B * (D_IN + D_H) * D_H

F32 = mybir.dt.float32
BF16 = mybir.dt.bfloat16
U32 = mybir.dt.uint32
U8 = mybir.dt.uint8
FP8 = mybir.dt.float8_e4m3fn
FP8X4 = mybir.dt.float8_e4m3fn_x4
ACT = mybir.ActivationFunctionType
ALU = mybir.AluOpType

P = 128
PACK = 4
ROW_TILES = B // P
CH_TILES = D_H // P
CHUNK = 256
HALF = 512
SHARE = 384
EPS = 1e-6
LN2 = 0.6931471805599453


def tile_slstmcell_pb_kernel(tc, x, h_prev, c, n, W_o_bytes, W_o_scale, b_o, U_o, out):
    nc = tc.nc
    with ExitStack() as ctx:
        keep = ctx.enter_context(tc.tile_pool(name="keep", bufs=1))
        rot = ctx.enter_context(tc.tile_pool(name="rot", bufs=3))
        psum = ctx.enter_context(tc.psum_pool(name="psum", bufs=8))
        ctx.enter_context(tc.manual_schedule())

        wsc = keep.tile([P, 2, PACK], F32, name="wsc")
        nc.scalar.dma_start(out=wsc[:], in_=W_o_scale.rearrange("(g p t) o -> p g (t o)", p=P, t=PACK))
        b_rows = keep.tile([P, P], BF16, name="b_rows")
        nc.gpsimd.memset(b_rows[:], 0.0)
        nc.scalar.dma_start(out=b_rows[0:CH_TILES, :], in_=b_o.rearrange("(j p) -> j p", p=P))
        one = keep.tile([P, 1], F32, name="one")
        nc.gpsimd.memset(one[:], 1.0)
        scratch = keep.tile([P, 1], F32, name="scratch")
        nc.scalar.activation(out=scratch[:], in_=one[:], func=ACT.Ln)
        ident_b = keep.tile([P, P], BF16, name="ident_b")
        make_identity(nc, ident_b[:])
        ident = keep.tile([P, P], F32, name="ident")
        make_identity(nc, ident[:])
        b_cols = psum.tile([P, P], BF16, name="b_cols", tag="bank")
        nc.tensor.transpose(b_cols[:], b_rows[:], ident_b[:])
        b_half = keep.tile([P, CH_TILES], F32, name="b_half")

        w_view = W_o_bytes.rearrange("(g p t) d -> g p t d", p=P, t=PACK)
        u_view = U_o.rearrange("(g p t) d -> g p t d", p=P, t=PACK)
        out_view = out.rearrange("(p i) d -> p i d", i=ROW_TILES)
        dram = {"x": x, "h": h_prev, "n": n, "c": c}
        w8 = [keep.tile([P, PACK, D_H], U8, name="w8_%d" % g) for g in range(2)]
        raw = [keep.tile([P, PACK, D_H], BF16, name="raw_%d" % q) for q in range(2)]
        raw_u = [[keep.tile([P, PACK, HALF], BF16, name="raw_u_%d_%d" % (g, hf)) for hf in range(2)] for g in range(2)]
        act_sb = {}
        for name in ("x", "h", "n", "c"):
            act_sb[name] = keep.tile([P, ROW_TILES, D_IN], BF16, name="%s_sb" % name)
        wg = [
            [keep.tile([P, HALF, PACK], BF16, name="wg_%d_%d" % (q, hf), align_bytes=64) for hf in range(2)]
            for q in range(4)
        ]
        wq = [keep.tile([P, D_H], U32, name="wq_%d" % q, align_bytes=64) for q in range(4)]
        ws = [keep.tile([P, D_H], U8, name="ws_%d" % q, align_bytes=64) for q in range(4)]
        xg = {}
        xq = {}
        xs = {}
        for name in ("x", "h"):
            xg[name] = keep.tile([P, 2 * B * PACK], BF16, name="xg_%s" % name, align_bytes=64)
            xq[name] = keep.tile([P, 2 * B], U32, name="xq_%s" % name, align_bytes=64)
            xs[name] = keep.tile([P, 2 * B], U8, name="xs_%s" % name, align_bytes=64)
        log_n = keep.tile([P, ROW_TILES, D_H], F32, name="log_n")
        recip = [keep.tile([P, ROW_TILES, CHUNK], F32, name="recip_%d" % k) for k in range(4)]
        ratio = [keep.tile([P, ROW_TILES, CHUNK], F32, name="ratio_%d" % k) for k in range(2)] + recip[0:2]
        o_sb = [keep.tile([P, ROW_TILES, CHUNK], F32, name="o_sb_%d" % k) for k in range(4)]
        banks = {}
        acc = {}
        gate_t = {}
        back = {}

        def load_w_plane(g, t):
            nc.sync.dma_start(out=w8[g][:, t, :], in_=w_view[g][:, t, :])

        def load_u(g, hf):
            cols = slice(hf * HALF, (hf + 1) * HALF)
            nc.sync.dma_start(out=raw_u[g][hf][:], in_=u_view[g][:, :, cols])

        def load_act(name, i0, i1):
            rows = slice(i0, i1)
            nc.sync.dma_start(
                out=act_sb[name][:, rows, :],
                in_=dram[name].rearrange("(p i) k -> p i k", i=ROW_TILES)[:, rows, :],
            )

        def widen_s(g, t):
            nc.scalar.activation(
                out=raw[g][:, t, :], in_=w8[g][:, t, :].bitcast(FP8), func=ACT.Copy, scale=wsc[:, g, t:t + 1]
            )

        def widen_v(g, t):
            nc.vector.tensor_scalar(
                out=raw[g][:, t, :],
                in0=w8[g][:, t, :].bitcast(FP8),
                scalar1=wsc[:, g, t:t + 1],
                scalar2=None,
                op0=ALU.mult,
            )

        def interleave(q, hf, copy, c0=0, c1=HALF):
            planes = raw[q][:, :, hf * HALF:(hf + 1) * HALF] if q < 2 else raw_u[q - 2][hf][:]
            copy(
                out=wg[q][hf][:, c0:c1, :].rearrange("p (c i) t -> p c t i", i=4),
                in_=planes[:, :, c0:c1].rearrange("p t (c i) -> p c t i", i=4),
            )

        def quant_w(q, hf):
            cols = slice(hf * HALF, (hf + 1) * HALF)
            nc.vector.quantize_mx(
                out=wq[q][:, cols].bitcast(FP8X4),
                scales=ws[q][:, cols],
                in_=wg[q][hf][:].rearrange("p d t -> p (d t)"),
            )

        def turn_act(name, g, rp):
            bank = psum.tile([P, 2, 2 * P], F32, name="bank", tag="bank")
            banks[(name, g, rp)] = bank
            warm(bank[:, 0, 0:P], 6 if (g, rp) == (0, 0) else 1)
            for ii in range(2):
                words = act_sb[name][:, 2 * rp + ii, :].bitcast(F32)
                for u in range(2):
                    nc.tensor.transpose(
                        bank[:, u, ii * P:(ii + 1) * P],
                        words[:, 256 * g + u:256 * (g + 1):2],
                        ident[:],
                    )

        def warm(out_cols, times):
            for i in range(times):
                nc.tensor.matmul(out_cols, lhsT=ident[:], rhs=ident[:], start=True, stop=True)

        def copy_act(name, g, rp):
            r0 = g * B + rp * 2 * P
            nc.scalar.copy(
                out=xg[name][:].bitcast(F32).rearrange("p (r u) -> p r u", u=2)[:, r0:r0 + 2 * P, :],
                in_=banks[(name, g, rp)][:].rearrange("p u r -> p r u"),
            )

        def quant_x(name):
            nc.vector.quantize_mx(out=xq[name][:].bitcast(FP8X4), scales=xs[name][:], in_=xg[name][:])

        def mx(q, hf, first, last):
            name = "x" if q < 2 else "h"
            toks = slice((q % 2) * B, (q % 2 + 1) * B)
            for j in range(4 * hf, 4 * hf + 4):
                if first:
                    acc[j] = psum.tile([P, B], F32, name="acc", tag="bank")
                cols = slice(j * P, (j + 1) * P)
                nc.tensor.matmul_mx(
                    out=acc[j][:],
                    lhsT=wq[q][:, cols].bitcast(FP8X4),
                    lhsT_scale=ws[q][:, cols],
                    rhs=xq[name][:, toks].bitcast(FP8X4),
                    rhs_scale=xs[name][:, toks],
                    start=first,
                    stop=last,
                )

        def tanh(j):
            gate_t[j] = rot.tile([P, B], F32, name="gate_t", tag="gate_t")
            nc.scalar.activation(out=gate_t[j][:], in_=acc[j][:], func=ACT.Tanh, bias=b_half[:, j:j + 1], scale=0.5)

        def turn_back(j):
            back[j] = psum.tile([P, ROW_TILES, P], F32, name="back", tag="bank")
            if j in (4, 5):
                warm(back[j][:, 0, :], 1)
            for i in range(ROW_TILES):
                nc.tensor.transpose(back[j][:, i, :], gate_t[j][:, i * P:(i + 1) * P], ident[:])

        def fin(j):
            k, jj = divmod(j, 2)
            nc.vector.scalar_tensor_tensor(
                out=o_sb[k][:, :, jj * P:(jj + 1) * P],
                in0=back[j][:],
                scalar=1.0,
                in1=ratio[k][:, :, jj * P:(jj + 1) * P],
                op0=ALU.add,
                op1=ALU.mult,
            )

        def store(k):
            nc.sync.dma_start(out=out_view[:, :, k * CHUNK:(k + 1) * CHUNK], in_=o_sb[k][:])

        def ln(rp):
            rows = slice(2 * rp, 2 * rp + 2)
            nc.scalar.activation(out=log_n[:, rows, :], in_=act_sb["n"][:, rows, :], func=ACT.Ln, bias=EPS, scale=1.0)

        def exp(k):
            nc.scalar.activation(
                out=recip[k][:], in_=log_n[:, :, k * CHUNK:(k + 1) * CHUNK], func=ACT.Exp, bias=-LN2, scale=-1.0
            )

        def rmul(k, engine):
            engine.tensor_tensor(
                out=ratio[k][:], in0=act_sb["c"][:, :, k * CHUNK:(k + 1) * CHUNK], in1=recip[k][:], op=ALU.mult
            )

        def rmul_tile(k, jj):
            cols = slice(jj * P, (jj + 1) * P)
            nc.gpsimd.tensor_tensor(
                out=ratio[k][:, :, cols],
                in0=act_sb["c"][:, :, (2 * k + jj) * P:(2 * k + jj + 1) * P],
                in1=recip[k][:, :, cols],
                op=ALU.mult,
            )

        for t in (2, 0, 3, 1):
            load_w_plane(0, t)
        for t in (2, 3, 1, 0):
            load_w_plane(1, t)
        load_act("x", 0, 2)
        load_act("x", 2, 4)
        load_act("n", 0, 2)
        load_act("h", 0, 4)
        load_u(0, 0)
        load_u(1, 0)
        load_act("n", 2, 4)
        load_u(0, 1)
        load_u(1, 1)
        load_act("c", 0, 4)

        for g, t in ((0, 0), (0, 1), (1, 0)):
            widen_s(g, t)
        for g, t in ((0, 2), (0, 3), (1, 2), (1, 3), (1, 1)):
            widen_v(g, t)
        interleave(0, 0, nc.vector.tensor_copy)
        interleave(0, 1, nc.vector.tensor_copy)
        interleave(1, 0, nc.vector.tensor_copy)
        interleave(1, 1, nc.scalar.copy, 0, SHARE)
        interleave(1, 1, nc.vector.tensor_copy, SHARE, HALF)
        nc.vector.tensor_scalar(out=b_half[:], in0=b_cols[:, 0:CH_TILES], scalar1=0.5, scalar2=None, op0=ALU.mult)
        for name in ("x", "h"):
            for rp in range(2):
                for g in range(2):
                    turn_act(name, g, rp)
        quant_w(0, 0)
        quant_w(0, 1)
        for rp in range(2):
            for g in range(2):
                copy_act("x", g, rp)
        quant_w(1, 0)
        quant_w(1, 1)
        ln(0)
        quant_x("x")
        mx(0, 0, True, False)
        mx(1, 0, False, False)
        for rp in range(2):
            for g in range(2):
                copy_act("h", g, rp)
        mx(0, 1, True, False)
        mx(1, 1, False, False)
        interleave(2, 0, nc.vector.tensor_copy)
        interleave(3, 0, nc.vector.tensor_copy)
        ln(1)
        quant_w(2, 0)
        quant_x("h")
        quant_w(3, 0)
        mx(2, 0, False, False)
        mx(3, 0, False, True)
        interleave(2, 1, nc.vector.tensor_copy)
        interleave(3, 1, nc.vector.tensor_copy)
        exp(0)
        exp(1)
        quant_w(2, 1)
        quant_w(3, 1)
        mx(2, 1, False, False)
        mx(3, 1, False, True)
        rmul(0, nc.vector)
        rmul(1, nc.vector)
        for k in range(4):
            for j in (2 * k, 2 * k + 1):
                tanh(j)
                turn_back(j)
            if k < 2:
                exp(k + 2)
                for jj in range(2):
                    rmul_tile(k + 2, jj)
            for j in (2 * k, 2 * k + 1):
                fin(j)
            store(k)
